import numpy as np
import ml_dtypes


def mxq(x, axis, fmt="e4m3"):
    dtype, down = {"e4m3": (ml_dtypes.float8_e4m3fn, 7), "e5m2": (ml_dtypes.float8_e5m2, 14)}[fmt]
    v = np.moveaxis(np.asarray(x, np.float32).astype(ml_dtypes.bfloat16).astype(np.float64), axis, -1)
    blocks = v.reshape(v.shape[:-1] + (-1, 32))
    amax = np.abs(blocks).max(-1, keepdims=True)
    byte = np.maximum(np.where(amax > 0, np.frexp(amax)[1] - 1 + 127, 0) - down, 1)
    scale = np.exp2(byte - 127.0)
    codes = (blocks / scale).astype(np.float32).astype(dtype).astype(np.float64)
    return np.moveaxis((codes * scale).reshape(v.shape), -1, axis)


WIDE = False


def mx_kscale(k):
    if not WIDE:
        return np.ones(k)
    levels = np.array([10, -10, 5, -5, 0])
    a = np.random.permutation(np.resize(levels, k // 512 * 4)).reshape(k // 512, 4)
    idx = np.arange(k)
    return np.exp2(a[idx // 512, idx % 128 // 32])


BF16 = ml_dtypes.bfloat16


def bf(x):
    return np.asarray(x, np.float32).astype(BF16)


def f64(x):
    return np.asarray(x).astype(np.float64)


E2M1 = np.array([0.0, 0.5, 1.0, 1.5, 2.0, 3.0, 4.0, 6.0, -0.0, -0.5, -1.0, -1.5, -2.0, -3.0, -4.0, -6.0])


def pack_weight(w, fmt):
    k, n = w.shape
    w = f64(bf(w)).reshape(k // 32, 32, n)
    amax = np.abs(w).max(1)
    if fmt == "e4m3":
        byte = np.frexp(amax)[1] - 1 + 127 - 7
    else:
        mant, ex = np.frexp(amax / 6.0)
        byte = np.where(mant > 0.5, ex, ex - 1) + 127
    byte = np.clip(np.where(amax > 0, byte, 1), 1, 254)
    scaled = (w * np.exp2(127.0 - byte)[:, None, :]).reshape(k, n).astype(np.float32)
    by_word = np.ascontiguousarray(scaled.reshape(k // 512, 128, 4, n).transpose(0, 1, 3, 2))
    if fmt == "e4m3":
        words = by_word.astype(ml_dtypes.float8_e4m3fn).view(np.uint8)
    else:
        c = by_word.astype(ml_dtypes.float4_e2m1fn).view(np.uint8) & 0xF
        words = c[..., 0::2] | (c[..., 1::2] << 4)
    return np.ascontiguousarray(words), np.ascontiguousarray(byte.astype(np.uint8).reshape(k // 512, 16, n))


def unpack_weight(words, scales, fmt):
    g, p, n, _ = words.shape
    if fmt == "e4m3":
        vals = np.ascontiguousarray(words).view(ml_dtypes.float8_e4m3fn).astype(np.float64)
    else:
        nib = np.empty((g, p, n, 4), np.uint8)
        nib[..., 0::2] = words & 0xF
        nib[..., 1::2] = words >> 4
        vals = E2M1[nib]
    vals = vals * np.repeat(np.exp2(scales.astype(np.float64) - 127.0), 8, axis=1)[..., None]
    return vals.transpose(0, 1, 3, 2).reshape(g * 512, n)


B, NF, GH, GW, DX, DIM, NH, CHUNK, SINK, MAXF = 1, 4, 8, 8, 16384, 1024, 8, 2, 1, 4
L = NF * GH * GW
HD = DIM // NH
C = HD // 2
DS = C // 3
DT = C - 2 * DS
MT = max(NF, GH, GW)
EPS = 1e-6


def rope_tables():
    def tab(d):
        inv = 1.0 / (10000.0 ** (np.arange(d) / d))
        ang = np.outer(np.arange(MT), inv)
        return np.cos(ang), np.sin(ang)
    ct, st = tab(DT)
    ch, sh = tab(DS)
    cw, sw = tab(DS)
    return np.concatenate([ct, ch, cw], axis=1), np.concatenate([st, sh, sw], axis=1)


def pos_table(tab):
    t = np.broadcast_to(tab[:NF, :DT][:, None, None, :], (NF, GH, GW, DT))
    hh = np.broadcast_to(tab[:GH, DT:DT + DS][None, :, None, :], (NF, GH, GW, DS))
    ww = np.broadcast_to(tab[:GW, DT + DS:][None, None, :, :], (NF, GH, GW, DS))
    return np.concatenate([t, hh, ww], axis=-1).reshape(L, C)


def setup_inputs():
    s = mx_kscale(DX)
    fc, fs = rope_tables()
    x = bf(np.random.standard_normal((B, L, DX)) * s)
    w = np.random.standard_normal((DIM, DX)) / np.sqrt(DX) / s[None, :]
    W_words, W_scales = pack_weight(np.ascontiguousarray(w.T), "e4m3")
    b = bf(np.random.standard_normal(DIM) * 0.3)
    g = bf(1.0 + 0.1 * np.random.standard_normal(DIM))
    return {"x": x,
            "W_words": W_words, "W_scales": W_scales,
            "b": b,
            "g": g,
            "freqs_cos": bf(fc), "freqs_sin": bf(fs)}


def reference(x, W_words, W_scales, b, g, freqs_cos, freqs_sin):
    y = (mxq(f64(x), 2, "e4m3") @ unpack_weight(W_words, W_scales, "e4m3")) + f64(b)
    z = y * (1.0 / np.sqrt(np.mean(y * y, axis=-1, keepdims=True) + EPS)) * f64(g)
    co = pos_table(f64(freqs_cos))[None, :, None, :]
    si = pos_table(f64(freqs_sin))[None, :, None, :]
    a = z.reshape(B, L, NH, C, 2)
    xr, xi = a[..., 0], a[..., 1]
    return np.stack([xr * co - xi * si, xr * si + xi * co], axis=-1).reshape(B, L, NH, HD)

@@ -1,0 +1,322 @@
+from contextlib import ExitStack
+
+import concourse.mybir as mybir
+from concourse.masks import make_identity
+
+F32 = mybir.dt.float32
+BF16 = mybir.dt.bfloat16
+I32 = mybir.dt.int32
+U32 = mybir.dt.uint32
+U8 = mybir.dt.uint8
+FP8X4 = mybir.dt.float8_e4m3fn_x4
+ALU = mybir.AluOpType
+ACT = mybir.ActivationFunctionType
+
+P = 128
+PACK = 4
+K_PASS = P * PACK
+TOKENS = 256
+K = 16384
+N = 1024
+EPS = 1e-6
+
+TOKEN_TILES = TOKENS // P
+BANK = 512
+N_BANKS = N // BANK
+PASSES = K // K_PASS
+CHUNK = 4
+CHUNKS = PASSES // CHUNK
+UNITS = TOKEN_TILES * CHUNK
+AHEAD = 2
+QUADRANTS = 4
+PLANE_ROWS = 4
+
+HEADS = 8
+PAIRS = 64
+M = HEADS * PAIRS
+M_BANK = BANK // 2
+GRID = 8
+FRAMES_PER_TILE = P // (GRID * GRID)
+FRAME_PAIRS = 22
+ROW_PAIRS = 43
+
+FLOPS = 2 * TOKENS * K * N
+
+
+def tile_causalwanselfattention_pa_k_kernel(
+    tc, x, W_words, W_scales, b, g, freqs_cos, freqs_sin, out
+):
+    nc = tc.nc
+    x_by_tile = x[0].rearrange("(i p) k -> p i k", p=P)
+    out_rows = out[0].rearrange("l h d -> l (h d)")
+
+    with ExitStack() as ctx:
+        consts = ctx.enter_context(tc.tile_pool(name="consts", bufs=1))
+        raw_pool = ctx.enter_context(tc.tile_pool(name="raw", bufs=3))
+        stage_pool = ctx.enter_context(tc.tile_pool(name="stage", bufs=2))
+        code_pool = ctx.enter_context(tc.tile_pool(name="codes", bufs=AHEAD + 2))
+        w_pool = ctx.enter_context(tc.tile_pool(name="w", bufs=3 * CHUNK))
+        tail_pool = ctx.enter_context(tc.tile_pool(name="tail", bufs=1))
+        acc_pool = ctx.enter_context(tc.psum_pool(name="acc", bufs=1))
+        bank_pool = ctx.enter_context(tc.psum_pool(name="bank", bufs=4))
+        ctx.enter_context(tc.manual_schedule())
+
+        w_scales = consts.tile([P, CHUNKS, N], U8, align_bytes=64)
+        nc.vector.memset(w_scales[:].rearrange("p c n -> p (c n)").bitcast(I32), 0)
+        bias_gain_row = consts.tile([P, 2 * N], BF16)
+        nc.vector.memset(bias_gain_row[:], 0.0)
+        freqs = consts.tile([P, 2 * PAIRS], BF16)
+        nc.vector.memset(freqs[:], 0.0)
+        ones = consts.tile([P, P], BF16)
+        nc.vector.memset(ones[:], 1.0)
+        eps = consts.tile([P, 1], F32)
+        nc.vector.memset(eps[:], EPS)
+        one_column = consts.tile([P, 1], F32)
+        nc.vector.memset(one_column[:], 1.0)
+        sqrt_of_one = consts.tile([P, 1], F32)
+        nc.scalar.activation(out=sqrt_of_one[:], in_=one_column[:], func=ACT.Sqrt)
+
+        ident = consts.tile([P, P], F32)
+        make_identity(nc, ident[:])
+        nc.gpsimd.dma_start(out=bias_gain_row[0:1, 0:N], in_=b.unsqueeze(0))
+        nc.gpsimd.dma_start(out=bias_gain_row[0:1, N : 2 * N], in_=g.unsqueeze(0))
+        nc.gpsimd.dma_start(out=freqs[0:GRID, 0:PAIRS], in_=freqs_cos)
+        nc.gpsimd.dma_start(out=freqs[0:GRID, PAIRS : 2 * PAIRS], in_=freqs_sin)
+
+        select = consts.tile([P, 4, P], BF16)
+        for i in range(TOKEN_TILES):
+            nc.vector.tensor_copy(
+                out=select[:, i, :].rearrange("p (f s) -> p f s", f=FRAMES_PER_TILE),
+                in_=ident[:, FRAMES_PER_TILE * i : FRAMES_PER_TILE * (i + 1)]
+                .unsqueeze(2)
+                .to_broadcast([P, FRAMES_PER_TILE, GRID * GRID]),
+            )
+        nc.vector.tensor_copy(
+            out=select[:, 2, :].rearrange("p (f r c) -> p f r c", f=FRAMES_PER_TILE, r=GRID),
+            in_=ident[:, 0:GRID]
+            .unsqueeze(1)
+            .unsqueeze(3)
+            .to_broadcast([P, FRAMES_PER_TILE, GRID, GRID]),
+        )
+        nc.vector.tensor_copy(
+            out=select[:, 3, :].rearrange("p (s c) -> p s c", c=GRID),
+            in_=ident[:, 0:GRID].unsqueeze(1).to_broadcast([P, P // GRID, GRID]),
+        )
+
+        acc = [
+            [
+                acc_pool.tile([P, BANK], F32, name="acc_%d_%d" % (i, h))
+                for h in range(N_BANKS)
+            ]
+            for i in range(TOKEN_TILES)
+        ]
+        x_raw = {}
+        x_codes = {}
+        x_scales = {}
+        w_codes = {}
+
+        def load_x_and_scales(c):
+            x_raw[c] = raw_pool.tile([P, TOKEN_TILES, CHUNK * K_PASS], BF16, name="x_raw")
+            k_cols = slice(c * CHUNK * K_PASS, (c + 1) * CHUNK * K_PASS)
+            nc.sync.dma_start(out=x_raw[c][:], in_=x_by_tile[:, :, k_cols])
+            for quadrant in range(QUADRANTS):
+                first = 32 * quadrant
+                rows = slice(PLANE_ROWS * quadrant, PLANE_ROWS * (quadrant + 1))
+                nc.sync.dma_start(
+                    out=w_scales[first : first + CHUNK * PLANE_ROWS, c, :].bitcast(I32),
+                    in_=W_scales[c * CHUNK : (c + 1) * CHUNK, rows, :].bitcast(I32),
+                )
+
+        def load_w(c):
+            for o in range(CHUNK):
+                k_pass = c * CHUNK + o
+                w_codes[k_pass] = w_pool.tile([P, PACK * N], U8, name="w_codes", align_bytes=64)
+                nc.sync.dma_start(
+                    out=w_codes[k_pass][:].bitcast(I32),
+                    in_=W_words[k_pass].rearrange("p n t -> p (n t)").bitcast(I32),
+                )
+
+        def prepare_x(c):
+            x_sorted = stage_pool.tile([P, UNITS, 2, P], F32)
+            nc.vector.tensor_copy(
+                out=x_sorted[:],
+                in_=x_raw[c][:]
+                .rearrange("p i k -> p (i k)")
+                .bitcast(F32)
+                .rearrange("p (a w u) -> p a u w", a=UNITS, u=2),
+            )
+            grouped = stage_pool.tile([P, UNITS, P, PACK], BF16, align_bytes=64)
+            for first_unit in range(0, UNITS, 2):
+                turned = bank_pool.tile([P, 4, P], F32, tag="bank")
+                for slot in range(4):
+                    nc.tensor.transpose(
+                        out=turned[:, slot, :],
+                        in_=x_sorted[:, first_unit + slot // 2, slot % 2, :],
+                        identity=ident[:],
+                    )
+                nc.scalar.copy(
+                    out=grouped[:, first_unit : first_unit + 2, :, :].bitcast(F32),
+                    in_=turned[:].rearrange("p (a u) r -> p a r u", u=2),
+                )
+            x_codes[c] = code_pool.tile([P, UNITS, P], U32, name="x_codes", align_bytes=64)
+            x_scales[c] = code_pool.tile([P, UNITS, P], U8, name="x_scales", align_bytes=64)
+            nc.vector.quantize_mx(
+                out=x_codes[c][:].rearrange("p a r -> p (a r)").bitcast(FP8X4),
+                scales=x_scales[c][:].rearrange("p a r -> p (a r)"),
+                in_=grouped[:].rearrange("p a r t -> p (a r t)"),
+            )
+
+        def multiply(c):
+            for o in range(CHUNK):
+                k_pass = c * CHUNK + o
+                for i in range(TOKEN_TILES):
+                    unit = i * CHUNK + o
+                    for h in range(N_BANKS):
+                        nc.tensor.matmul_mx(
+                            out=acc[i][h][:],
+                            lhsT=x_codes[c][:, unit, :].bitcast(FP8X4),
+                            lhsT_scale=x_scales[c][:, unit, :],
+                            rhs=w_codes[k_pass][:, PACK * BANK * h : PACK * BANK * (h + 1)].bitcast(
+                                FP8X4
+                            ),
+                            rhs_scale=w_scales[PLANE_ROWS * o : P, c, BANK * h : BANK * (h + 1)],
+                            start=(k_pass == 0),
+                            stop=(k_pass == PASSES - 1),
+                        )
+
+        bias_gain = consts.tile([P, 2, 2, M], F32)
+        cos_sin = consts.tile([P, TOKEN_TILES, 3, PAIRS], F32)
+        own_factor = consts.tile([P, TOKEN_TILES, 2, M], F32)
+        partner_factor = consts.tile([P, TOKEN_TILES, 2, M], F32)
+
+        def build_tables():
+            for q in range(2 * N_BANKS):
+                spread = bank_pool.tile([P, BANK], F32, tag="bank")
+                nc.tensor.matmul(
+                    out=spread[:],
+                    lhsT=ones[:],
+                    rhs=bias_gain_row[:, BANK * q : BANK * (q + 1)],
+                    start=True,
+                    stop=True,
+                )
+                half = q % N_BANKS
+                nc.scalar.copy(
+                    out=bias_gain[:, q // N_BANKS, :, M_BANK * half : M_BANK * (half + 1)],
+                    in_=spread[:].rearrange("p (m e) -> p e m", e=2),
+                )
+            picked = bank_pool.tile([P, 4, 2, PAIRS], F32, tag="bank")
+            for s in range(4):
+                nc.tensor.matmul(
+                    out=picked[:, s, :, :].rearrange("p s j -> p (s j)"),
+                    lhsT=select[:, s, :],
+                    rhs=freqs[:],
+                    start=True,
+                    stop=True,
+                )
+            gain = bias_gain[:, 1, :, :]
+            for i in range(TOKEN_TILES):
+                for s, first, last in (
+                    (i, 0, FRAME_PAIRS),
+                    (2, FRAME_PAIRS, ROW_PAIRS),
+                    (3, ROW_PAIRS, PAIRS),
+                ):
+                    nc.vector.tensor_copy(
+                        out=cos_sin[:, i, 0:2, first:last], in_=picked[:, s, :, first:last]
+                    )
+                nc.vector.tensor_scalar_mul(
+                    out=cos_sin[:, i, 2, :], in0=cos_sin[:, i, 1, :], scalar1=-1.0
+                )
+                nc.vector.tensor_tensor(
+                    out=own_factor[:, i, :, :].rearrange("p e (h j) -> p (e h) j", j=PAIRS),
+                    in0=gain.rearrange("p e (h j) -> p (e h) j", j=PAIRS),
+                    in1=cos_sin[:, i, 0:1, :].to_broadcast([P, 2 * HEADS, PAIRS]),
+                    op=ALU.mult,
+                )
+                for e in range(2):
+                    nc.vector.tensor_tensor(
+                        out=partner_factor[:, i, e, :].rearrange("p (h j) -> p h j", j=PAIRS),
+                        in0=gain[:, 1 - e, :].rearrange("p (h j) -> p h j", j=PAIRS),
+                        in1=cos_sin[:, i, 2 - e : 3 - e, :].to_broadcast([P, HEADS, PAIRS]),
+                        op=ALU.mult,
+                    )
+
+        y = {}
+        rms = {}
+        own = {}
+
+        def add_bias_and_measure(i):
+            y[i] = tail_pool.tile([P, 2, M], F32, name="y_%d" % i)
+            for h in range(N_BANKS):
+                pairs = slice(M_BANK * h, M_BANK * (h + 1))
+                nc.vector.tensor_tensor(
+                    out=y[i][:, :, pairs],
+                    in0=acc[i][h][:].rearrange("p (m e) -> p e m", e=2),
+                    in1=bias_gain[:, 0, :, pairs],
+                    op=ALU.add,
+                )
+            squares = tail_pool.tile([P, N], F32, name="squares_%d" % i)
+            sum_squares = tail_pool.tile([P, 1], F32, name="sum_squares_%d" % i)
+            nc.scalar.activation(
+                out=squares[:],
+                in_=y[i][:].rearrange("p e m -> p (e m)"),
+                func=ACT.Square,
+                accum_out=sum_squares[:],
+            )
+            rms[i] = tail_pool.tile([P, 1], F32, name="rms_%d" % i)
+            nc.scalar.activation(
+                out=rms[i][:], in_=sum_squares[:], func=ACT.Sqrt, scale=1.0 / N, bias=eps[:]
+            )
+
+        def multiply_own(i):
+            own[i] = tail_pool.tile([P, 2, M], F32, name="own_%d" % i)
+            nc.vector.tensor_tensor(
+                out=own[i][:].rearrange("p e m -> p (e m)"),
+                in0=y[i][:].rearrange("p e m -> p (e m)"),
+                in1=own_factor[:, i, :, :].rearrange("p e m -> p (e m)"),
+                op=ALU.mult,
+            )
+
+        def rotate_and_store(i):
+            inv_rms = tail_pool.tile([P, 1], F32, name="inv_rms_%d" % i)
+            nc.vector.reciprocal(out=inv_rms[:], in_=rms[i][:])
+            partner = tail_pool.tile([P, 2, M], F32, name="partner_%d" % i)
+            for e in range(2):
+                nc.vector.scalar_tensor_tensor(
+                    out=partner[:, e, :],
+                    in0=y[i][:, 1 - e, :],
+                    scalar=inv_rms[:],
+                    in1=partner_factor[:, i, e, :],
+                    op0=ALU.mult,
+                    op1=ALU.mult,
+                )
+            result = tail_pool.tile([P, N], F32, name="result_%d" % i)
+            for h in range(N_BANKS):
+                pairs = slice(M_BANK * h, M_BANK * (h + 1))
+                n_cols = slice(BANK * h, BANK * (h + 1))
+                nc.vector.scalar_tensor_tensor(
+                    out=result[:, n_cols].rearrange("p (m e) -> p m e", e=2),
+                    in0=own[i][:, :, pairs].rearrange("p e m -> p m e"),
+                    scalar=inv_rms[:],
+                    in1=partner[:, :, pairs].rearrange("p e m -> p m e"),
+                    op0=ALU.mult,
+                    op1=ALU.add,
+                )
+                nc.sync.dma_start(out=out_rows[P * i : P * (i + 1), n_cols], in_=result[:, n_cols])
+
+        for c in range(AHEAD):
+            load_x_and_scales(c)
+            prepare_x(c)
+        build_tables()
+        for c in range(CHUNKS):
+            if c + AHEAD < CHUNKS:
+                load_x_and_scales(c + AHEAD)
+            load_w(c)
+            multiply(c)
+            if c + AHEAD < CHUNKS:
+                prepare_x(c + AHEAD)
+        for i in range(TOKEN_TILES):
+            add_bias_and_measure(i)
+        for i in range(TOKEN_TILES):
+            multiply_own(i)
+        for i in range(TOKEN_TILES):
+            rotate_and_store(i)

@@ -67,6 +67,10 @@ def tile_causalwanselfattention_pa_k_kernel(
         nc.vector.memset(bias_gain_row[:], 0.0)
         freqs = consts.tile([P, 2 * PAIRS], BF16)
         nc.vector.memset(freqs[:], 0.0)
+        nc.scalar.dma_start(out=bias_gain_row[0:1, 0:N], in_=b.unsqueeze(0))
+        nc.scalar.dma_start(out=bias_gain_row[0:1, N : 2 * N], in_=g.unsqueeze(0))
+        nc.scalar.dma_start(out=freqs[0:GRID, 0:PAIRS], in_=freqs_cos)
+        nc.scalar.dma_start(out=freqs[0:GRID, PAIRS : 2 * PAIRS], in_=freqs_sin)
         ones = consts.tile([P, P], BF16)
         nc.vector.memset(ones[:], 1.0)
         eps = consts.tile([P, 1], F32)
@@ -78,10 +82,15 @@ def tile_causalwanselfattention_pa_k_kernel(
 
         ident = consts.tile([P, P], F32)
         make_identity(nc, ident[:])
-        nc.gpsimd.dma_start(out=bias_gain_row[0:1, 0:N], in_=b.unsqueeze(0))
-        nc.gpsimd.dma_start(out=bias_gain_row[0:1, N : 2 * N], in_=g.unsqueeze(0))
-        nc.gpsimd.dma_start(out=freqs[0:GRID, 0:PAIRS], in_=freqs_cos)
-        nc.gpsimd.dma_start(out=freqs[0:GRID, PAIRS : 2 * PAIRS], in_=freqs_sin)
+
+        for c in range(CHUNKS):
+            for quadrant in range(QUADRANTS):
+                first = 32 * quadrant
+                rows = slice(PLANE_ROWS * quadrant, PLANE_ROWS * (quadrant + 1))
+                nc.gpsimd.dma_start(
+                    out=w_scales[first : first + CHUNK * PLANE_ROWS, c, :].bitcast(F32),
+                    in_=W_scales[c * CHUNK : (c + 1) * CHUNK, rows, :].bitcast(F32),
+                )
 
         select = consts.tile([P, 4, P], BF16)
         for i in range(TOKEN_TILES):
@@ -115,17 +124,10 @@ def tile_causalwanselfattention_pa_k_kernel(
         x_scales = {}
         w_codes = {}
 
-        def load_x_and_scales(c):
+        def load_x(c):
             x_raw[c] = raw_pool.tile([P, TOKEN_TILES, CHUNK * K_PASS], BF16, name="x_raw")
             k_cols = slice(c * CHUNK * K_PASS, (c + 1) * CHUNK * K_PASS)
             nc.sync.dma_start(out=x_raw[c][:], in_=x_by_tile[:, :, k_cols])
-            for quadrant in range(QUADRANTS):
-                first = 32 * quadrant
-                rows = slice(PLANE_ROWS * quadrant, PLANE_ROWS * (quadrant + 1))
-                nc.sync.dma_start(
-                    out=w_scales[first : first + CHUNK * PLANE_ROWS, c, :].bitcast(I32),
-                    in_=W_scales[c * CHUNK : (c + 1) * CHUNK, rows, :].bitcast(I32),
-                )
 
         def load_w(c):
             for o in range(CHUNK):
@@ -304,12 +306,12 @@ def tile_causalwanselfattention_pa_k_kernel(
                 nc.sync.dma_start(out=out_rows[P * i : P * (i + 1), n_cols], in_=result[:, n_cols])
 
         for c in range(AHEAD):
-            load_x_and_scales(c)
+            load_x(c)
             prepare_x(c)
         build_tables()
         for c in range(CHUNKS):
             if c + AHEAD < CHUNKS:
-                load_x_and_scales(c + AHEAD)
+                load_x(c + AHEAD)
             load_w(c)
             multiply(c)
             if c + AHEAD < CHUNKS:

@@ -27,7 +27,9 @@ PASSES = K // K_PASS
 CHUNK = 4
 CHUNKS = PASSES // CHUNK
 UNITS = TOKEN_TILES * CHUNK
-AHEAD = 2
+SPLIT = CHUNKS // 2
+LOAD_AHEAD = 3
+TURN_AHEAD = 2
 QUADRANTS = 4
 PLANE_ROWS = 4
 
@@ -54,7 +56,7 @@ def tile_causalwanselfattention_pa_k_kernel(
         consts = ctx.enter_context(tc.tile_pool(name="consts", bufs=1))
         raw_pool = ctx.enter_context(tc.tile_pool(name="raw", bufs=3))
         stage_pool = ctx.enter_context(tc.tile_pool(name="stage", bufs=2))
-        code_pool = ctx.enter_context(tc.tile_pool(name="codes", bufs=AHEAD + 2))
+        code_pool = ctx.enter_context(tc.tile_pool(name="codes", bufs=CHUNKS - SPLIT))
         w_pool = ctx.enter_context(tc.tile_pool(name="w", bufs=3 * CHUNK))
         tail_pool = ctx.enter_context(tc.tile_pool(name="tail", bufs=1))
         acc_pool = ctx.enter_context(tc.psum_pool(name="acc", bufs=1))
@@ -73,8 +75,6 @@ def tile_causalwanselfattention_pa_k_kernel(
         nc.scalar.dma_start(out=freqs[0:GRID, PAIRS : 2 * PAIRS], in_=freqs_sin)
         ones = consts.tile([P, P], BF16)
         nc.vector.memset(ones[:], 1.0)
-        eps = consts.tile([P, 1], F32)
-        nc.vector.memset(eps[:], EPS)
         one_column = consts.tile([P, 1], F32)
         nc.vector.memset(one_column[:], 1.0)
         sqrt_of_one = consts.tile([P, 1], F32)
@@ -120,43 +120,38 @@ def tile_causalwanselfattention_pa_k_kernel(
             for i in range(TOKEN_TILES)
         ]
         x_raw = {}
+        x_sorted = {}
         x_codes = {}
         x_scales = {}
-        w_codes = {}
 
         def load_x(c):
             x_raw[c] = raw_pool.tile([P, TOKEN_TILES, CHUNK * K_PASS], BF16, name="x_raw")
             k_cols = slice(c * CHUNK * K_PASS, (c + 1) * CHUNK * K_PASS)
             nc.sync.dma_start(out=x_raw[c][:], in_=x_by_tile[:, :, k_cols])
 
-        def load_w(c):
-            for o in range(CHUNK):
-                k_pass = c * CHUNK + o
-                w_codes[k_pass] = w_pool.tile([P, PACK * N], U8, name="w_codes", align_bytes=64)
-                nc.sync.dma_start(
-                    out=w_codes[k_pass][:].bitcast(I32),
-                    in_=W_words[k_pass].rearrange("p n t -> p (n t)").bitcast(I32),
-                )
-
-        def prepare_x(c):
-            x_sorted = stage_pool.tile([P, UNITS, 2, P], F32)
+        def sort_x(c):
+            x_sorted[c] = stage_pool.tile([P, UNITS, 2, P], F32, name="x_sorted")
             nc.vector.tensor_copy(
-                out=x_sorted[:],
+                out=x_sorted[c][:],
                 in_=x_raw[c][:]
                 .rearrange("p i k -> p (i k)")
                 .bitcast(F32)
                 .rearrange("p (a w u) -> p a u w", a=UNITS, u=2),
             )
+
+        def turn_and_quantise_x(c):
             grouped = stage_pool.tile([P, UNITS, P, PACK], BF16, align_bytes=64)
-            for first_unit in range(0, UNITS, 2):
+            for bank in range(UNITS // 2):
+                first_unit = 2 * bank
                 turned = bank_pool.tile([P, 4, P], F32, tag="bank")
                 for slot in range(4):
                     nc.tensor.transpose(
                         out=turned[:, slot, :],
-                        in_=x_sorted[:, first_unit + slot // 2, slot % 2, :],
+                        in_=x_sorted[c][:, first_unit + slot // 2, slot % 2, :],
                         identity=ident[:],
                     )
-                nc.scalar.copy(
+                copy_out = nc.scalar.copy if bank % 2 == 0 else nc.vector.tensor_copy
+                copy_out(
                     out=grouped[:, first_unit : first_unit + 2, :, :].bitcast(F32),
                     in_=turned[:].rearrange("p (a u) r -> p a r u", u=2),
                 )
@@ -168,19 +163,38 @@ def tile_causalwanselfattention_pa_k_kernel(
                 in_=grouped[:].rearrange("p a r t -> p (a r t)"),
             )
 
-        def multiply(c):
+        def load_w(c, first_bank, n_banks):
+            n_passes = N_BANKS // n_banks
+            byte_cols = slice(first_bank * PACK * BANK, (first_bank + n_banks) * PACK * BANK)
+            pieces = []
+            for first_pass in range(c * CHUNK, (c + 1) * CHUNK, n_passes):
+                piece = w_pool.tile(
+                    [P, n_passes, n_banks * PACK * BANK], U8, name="w_codes", align_bytes=64
+                )
+                nc.sync.dma_start(
+                    out=piece[:].bitcast(I32),
+                    in_=W_words[first_pass : first_pass + n_passes]
+                    .rearrange("g p n t -> p g (n t)")[:, :, byte_cols]
+                    .bitcast(I32),
+                )
+                pieces.append(piece)
+            return pieces
+
+        def multiply(c, pieces, first_bank, n_banks):
+            n_passes = N_BANKS // n_banks
             for o in range(CHUNK):
                 k_pass = c * CHUNK + o
+                piece = pieces[o // n_passes]
                 for i in range(TOKEN_TILES):
                     unit = i * CHUNK + o
-                    for h in range(N_BANKS):
+                    for local_bank in range(n_banks):
+                        h = first_bank + local_bank
+                        byte_cols = slice(local_bank * PACK * BANK, (local_bank + 1) * PACK * BANK)
                         nc.tensor.matmul_mx(
                             out=acc[i][h][:],
                             lhsT=x_codes[c][:, unit, :].bitcast(FP8X4),
                             lhsT_scale=x_scales[c][:, unit, :],
-                            rhs=w_codes[k_pass][:, PACK * BANK * h : PACK * BANK * (h + 1)].bitcast(
-                                FP8X4
-                            ),
+                            rhs=piece[:, o % n_passes, byte_cols].bitcast(FP8X4),
                             rhs_scale=w_scales[PLANE_ROWS * o : P, c, BANK * h : BANK * (h + 1)],
                             start=(k_pass == 0),
                             stop=(k_pass == PASSES - 1),
@@ -243,82 +257,123 @@ def tile_causalwanselfattention_pa_k_kernel(
                     )
 
         y = {}
-        rms = {}
+        sum_squares = {}
         own = {}
+        rotated = {}
+        inv_rms = {}
 
-        def add_bias_and_measure(i):
-            y[i] = tail_pool.tile([P, 2, M], F32, name="y_%d" % i)
-            for h in range(N_BANKS):
-                pairs = slice(M_BANK * h, M_BANK * (h + 1))
-                nc.vector.tensor_tensor(
-                    out=y[i][:, :, pairs],
-                    in0=acc[i][h][:].rearrange("p (m e) -> p e m", e=2),
-                    in1=bias_gain[:, 0, :, pairs],
-                    op=ALU.add,
-                )
-            squares = tail_pool.tile([P, N], F32, name="squares_%d" % i)
-            sum_squares = tail_pool.tile([P, 1], F32, name="sum_squares_%d" % i)
+        def add_bias_and_square(i, h):
+            pairs = slice(M_BANK * h, M_BANK * (h + 1))
+            y[i, h] = tail_pool.tile([P, 2, M_BANK], F32, name="y_%d_%d" % (i, h))
+            nc.vector.tensor_tensor(
+                out=y[i, h][:],
+                in0=acc[i][h][:].rearrange("p (m e) -> p e m", e=2),
+                in1=bias_gain[:, 0, :, pairs],
+                op=ALU.add,
+            )
+            squares = tail_pool.tile([P, BANK], F32, name="squares_%d_%d" % (i, h))
+            sum_squares[i, h] = tail_pool.tile([P, 1], F32, name="sum_squares_%d_%d" % (i, h))
             nc.scalar.activation(
                 out=squares[:],
-                in_=y[i][:].rearrange("p e m -> p (e m)"),
+                in_=y[i, h][:].rearrange("p e m -> p (e m)"),
                 func=ACT.Square,
-                accum_out=sum_squares[:],
-            )
-            rms[i] = tail_pool.tile([P, 1], F32, name="rms_%d" % i)
-            nc.scalar.activation(
-                out=rms[i][:], in_=sum_squares[:], func=ACT.Sqrt, scale=1.0 / N, bias=eps[:]
+                accum_out=sum_squares[i, h][:],
             )
 
-        def multiply_own(i):
-            own[i] = tail_pool.tile([P, 2, M], F32, name="own_%d" % i)
+        def multiply_own(i, h):
+            pairs = slice(M_BANK * h, M_BANK * (h + 1))
+            own[i, h] = tail_pool.tile([P, 2, M_BANK], F32, name="own_%d_%d" % (i, h))
             nc.vector.tensor_tensor(
-                out=own[i][:].rearrange("p e m -> p (e m)"),
-                in0=y[i][:].rearrange("p e m -> p (e m)"),
-                in1=own_factor[:, i, :, :].rearrange("p e m -> p (e m)"),
-                op=ALU.mult,
+                out=own[i, h][:], in0=y[i, h][:], in1=own_factor[:, i, :, pairs], op=ALU.mult
             )
 
-        def rotate_and_store(i):
-            inv_rms = tail_pool.tile([P, 1], F32, name="inv_rms_%d" % i)
-            nc.vector.reciprocal(out=inv_rms[:], in_=rms[i][:])
-            partner = tail_pool.tile([P, 2, M], F32, name="partner_%d" % i)
+        def rotate(i, h, factor):
+            pairs = slice(M_BANK * h, M_BANK * (h + 1))
+            partner = tail_pool.tile([P, 2, M_BANK], F32, name="partner_%d_%d" % (i, h))
             for e in range(2):
                 nc.vector.scalar_tensor_tensor(
                     out=partner[:, e, :],
-                    in0=y[i][:, 1 - e, :],
-                    scalar=inv_rms[:],
-                    in1=partner_factor[:, i, e, :],
+                    in0=y[i, h][:, 1 - e, :],
+                    scalar=factor,
+                    in1=partner_factor[:, i, e, pairs],
                     op0=ALU.mult,
                     op1=ALU.mult,
                 )
-            result = tail_pool.tile([P, N], F32, name="result_%d" % i)
-            for h in range(N_BANKS):
-                pairs = slice(M_BANK * h, M_BANK * (h + 1))
-                n_cols = slice(BANK * h, BANK * (h + 1))
-                nc.vector.scalar_tensor_tensor(
-                    out=result[:, n_cols].rearrange("p (m e) -> p m e", e=2),
-                    in0=own[i][:, :, pairs].rearrange("p e m -> p m e"),
-                    scalar=inv_rms[:],
-                    in1=partner[:, :, pairs].rearrange("p e m -> p m e"),
-                    op0=ALU.mult,
-                    op1=ALU.add,
-                )
-                nc.sync.dma_start(out=out_rows[P * i : P * (i + 1), n_cols], in_=result[:, n_cols])
+            rotated[i, h] = tail_pool.tile([P, BANK], F32, name="rotated_%d_%d" % (i, h))
+            nc.vector.scalar_tensor_tensor(
+                out=rotated[i, h][:].rearrange("p (m e) -> p m e", e=2),
+                in0=own[i, h][:].rearrange("p e m -> p m e"),
+                scalar=factor,
+                in1=partner[:].rearrange("p e m -> p m e"),
+                op0=ALU.mult,
+                op1=ALU.add,
+            )
 
-        for c in range(AHEAD):
+        def store(i, h, result):
+            nc.sync.dma_start(
+                out=out_rows[P * i : P * (i + 1), BANK * h : BANK * (h + 1)], in_=result[:]
+            )
+
+        for c in range(LOAD_AHEAD):
             load_x(c)
-            prepare_x(c)
+        sort_x(0)
+        for c in range(TURN_AHEAD):
+            sort_x(c + 1)
+            turn_and_quantise_x(c)
         build_tables()
+
         for c in range(CHUNKS):
-            if c + AHEAD < CHUNKS:
-                load_x(c + AHEAD)
-            load_w(c)
-            multiply(c)
-            if c + AHEAD < CHUNKS:
-                prepare_x(c + AHEAD)
+            n_banks = N_BANKS if c < SPLIT else 1
+            pieces = load_w(c, 0, n_banks)
+            if c + LOAD_AHEAD < CHUNKS:
+                load_x(c + LOAD_AHEAD)
+            multiply(c, pieces, 0, n_banks)
+            if c + LOAD_AHEAD < CHUNKS:
+                sort_x(c + LOAD_AHEAD)
+            if c + TURN_AHEAD < CHUNKS:
+                turn_and_quantise_x(c + TURN_AHEAD)
+
+        early_mean = {}
         for i in range(TOKEN_TILES):
-            add_bias_and_measure(i)
+            add_bias_and_square(i, 0)
         for i in range(TOKEN_TILES):
-            multiply_own(i)
+            multiply_own(i, 0)
+            rotate(i, 0, 1.0)
+            early_mean[i] = tail_pool.tile([P, 1], F32, name="early_mean_%d" % i)
+            nc.vector.tensor_scalar(
+                out=early_mean[i][:],
+                in0=sum_squares[i, 0][:],
+                scalar1=1.0 / N,
+                scalar2=EPS,
+                op0=ALU.mult,
+                op1=ALU.add,
+            )
+
+        for c in range(SPLIT, CHUNKS):
+            pieces = load_w(c, 1, 1)
+            multiply(c, pieces, 1, 1)
+
         for i in range(TOKEN_TILES):
-            rotate_and_store(i)
+            add_bias_and_square(i, 1)
+        for i in range(TOKEN_TILES):
+            multiply_own(i, 1)
+        for i in range(TOKEN_TILES):
+            rms = tail_pool.tile([P, 1], F32, name="rms_%d" % i)
+            nc.scalar.activation(
+                out=rms[:],
+                in_=sum_squares[i, 1][:],
+                func=ACT.Sqrt,
+                scale=1.0 / N,
+                bias=early_mean[i][:],
+            )
+            inv_rms[i] = tail_pool.tile([P, 1], F32, name="inv_rms_%d" % i)
+            nc.vector.reciprocal(out=inv_rms[i][:], in_=rms[:])
+        for i in range(TOKEN_TILES):
+            scaled = tail_pool.tile([P, BANK], F32, name="scaled_%d" % i)
+            nc.scalar.activation(
+                out=scaled[:], in_=rotated[i, 0][:], func=ACT.Copy, scale=inv_rms[i][:]
+            )
+            store(i, 0, scaled)
+        for i in range(TOKEN_TILES):
+            rotate(i, 1, inv_rms[i][:])
+            store(i, 1, rotated[i, 1])

@@ -27,7 +27,7 @@ PASSES = K // K_PASS
 CHUNK = 4
 CHUNKS = PASSES // CHUNK
 UNITS = TOKEN_TILES * CHUNK
-SPLIT = CHUNKS // 2
+SPLIT = 5
 LOAD_AHEAD = 3
 TURN_AHEAD = 2
 QUADRANTS = 4
@@ -56,7 +56,7 @@ def tile_causalwanselfattention_pa_k_kernel(
         consts = ctx.enter_context(tc.tile_pool(name="consts", bufs=1))
         raw_pool = ctx.enter_context(tc.tile_pool(name="raw", bufs=3))
         stage_pool = ctx.enter_context(tc.tile_pool(name="stage", bufs=2))
-        code_pool = ctx.enter_context(tc.tile_pool(name="codes", bufs=CHUNKS - SPLIT))
+        code_pool = ctx.enter_context(tc.tile_pool(name="codes", bufs=TURN_AHEAD + 2))
         w_pool = ctx.enter_context(tc.tile_pool(name="w", bufs=3 * CHUNK))
         tail_pool = ctx.enter_context(tc.tile_pool(name="tail", bufs=1))
         acc_pool = ctx.enter_context(tc.psum_pool(name="acc", bufs=1))
@@ -164,27 +164,20 @@ def tile_causalwanselfattention_pa_k_kernel(
             )
 
         def load_w(c, first_bank, n_banks):
-            n_passes = N_BANKS // n_banks
             byte_cols = slice(first_bank * PACK * BANK, (first_bank + n_banks) * PACK * BANK)
             pieces = []
-            for first_pass in range(c * CHUNK, (c + 1) * CHUNK, n_passes):
-                piece = w_pool.tile(
-                    [P, n_passes, n_banks * PACK * BANK], U8, name="w_codes", align_bytes=64
-                )
+            for k_pass in range(c * CHUNK, (c + 1) * CHUNK):
+                piece = w_pool.tile([P, n_banks * PACK * BANK], U8, name="w_codes", align_bytes=64)
                 nc.sync.dma_start(
                     out=piece[:].bitcast(I32),
-                    in_=W_words[first_pass : first_pass + n_passes]
-                    .rearrange("g p n t -> p g (n t)")[:, :, byte_cols]
-                    .bitcast(I32),
+                    in_=W_words[k_pass].rearrange("p n t -> p (n t)")[:, byte_cols].bitcast(I32),
                 )
                 pieces.append(piece)
             return pieces
 
         def multiply(c, pieces, first_bank, n_banks):
-            n_passes = N_BANKS // n_banks
             for o in range(CHUNK):
                 k_pass = c * CHUNK + o
-                piece = pieces[o // n_passes]
                 for i in range(TOKEN_TILES):
                     unit = i * CHUNK + o
                     for local_bank in range(n_banks):
@@ -194,7 +187,7 @@ def tile_causalwanselfattention_pa_k_kernel(
                             out=acc[i][h][:],
                             lhsT=x_codes[c][:, unit, :].bitcast(FP8X4),
                             lhsT_scale=x_scales[c][:, unit, :],
-                            rhs=piece[:, o % n_passes, byte_cols].bitcast(FP8X4),
+                            rhs=pieces[o][:, byte_cols].bitcast(FP8X4),
                             rhs_scale=w_scales[PLANE_ROWS * o : P, c, BANK * h : BANK * (h + 1)],
                             start=(k_pass == 0),
                             stop=(k_pass == PASSES - 1),

@@ -121,6 +121,7 @@ def tile_causalwanselfattention_pa_k_kernel(
         ]
         x_raw = {}
         x_sorted = {}
+        grouped = {}
         x_codes = {}
         x_scales = {}
 
@@ -139,10 +140,11 @@ def tile_causalwanselfattention_pa_k_kernel(
                 .rearrange("p (a w u) -> p a u w", a=UNITS, u=2),
             )
 
-        def turn_and_quantise_x(c):
-            grouped = stage_pool.tile([P, UNITS, P, PACK], BF16, align_bytes=64)
-            for bank in range(UNITS // 2):
-                first_unit = 2 * bank
+        def turn_x(c, i):
+            if i == 0:
+                grouped[c] = stage_pool.tile([P, UNITS, P, PACK], BF16, name="grouped", align_bytes=64)
+            for half in range(2):
+                first_unit = i * CHUNK + 2 * half
                 turned = bank_pool.tile([P, 4, P], F32, tag="bank")
                 for slot in range(4):
                     nc.tensor.transpose(
@@ -150,17 +152,19 @@ def tile_causalwanselfattention_pa_k_kernel(
                         in_=x_sorted[c][:, first_unit + slot // 2, slot % 2, :],
                         identity=ident[:],
                     )
-                copy_out = nc.scalar.copy if bank % 2 == 0 else nc.vector.tensor_copy
+                copy_out = nc.scalar.copy if half == 0 else nc.vector.tensor_copy
                 copy_out(
-                    out=grouped[:, first_unit : first_unit + 2, :, :].bitcast(F32),
+                    out=grouped[c][:, first_unit : first_unit + 2, :, :].bitcast(F32),
                     in_=turned[:].rearrange("p (a u) r -> p a r u", u=2),
                 )
+
+        def quantise_x(c):
             x_codes[c] = code_pool.tile([P, UNITS, P], U32, name="x_codes", align_bytes=64)
             x_scales[c] = code_pool.tile([P, UNITS, P], U8, name="x_scales", align_bytes=64)
             nc.vector.quantize_mx(
                 out=x_codes[c][:].rearrange("p a r -> p (a r)").bitcast(FP8X4),
                 scales=x_scales[c][:].rearrange("p a r -> p (a r)"),
-                in_=grouped[:].rearrange("p a r t -> p (a r t)"),
+                in_=grouped[c][:].rearrange("p a r t -> p (a r t)"),
             )
 
         def load_w(c, first_bank, n_banks):
@@ -175,8 +179,8 @@ def tile_causalwanselfattention_pa_k_kernel(
                 pieces.append(piece)
             return pieces
 
-        def multiply(c, pieces, first_bank, n_banks):
-            for o in range(CHUNK):
+        def multiply(c, pieces, first_bank, n_banks, passes=range(CHUNK)):
+            for o in passes:
                 k_pass = c * CHUNK + o
                 for i in range(TOKEN_TILES):
                     unit = i * CHUNK + o
@@ -312,7 +316,9 @@ def tile_causalwanselfattention_pa_k_kernel(
         sort_x(0)
         for c in range(TURN_AHEAD):
             sort_x(c + 1)
-            turn_and_quantise_x(c)
+            for i in range(TOKEN_TILES):
+                turn_x(c, i)
+            quantise_x(c)
         build_tables()
 
         for c in range(CHUNKS):
@@ -320,11 +326,14 @@ def tile_causalwanselfattention_pa_k_kernel(
             pieces = load_w(c, 0, n_banks)
             if c + LOAD_AHEAD < CHUNKS:
                 load_x(c + LOAD_AHEAD)
-            multiply(c, pieces, 0, n_banks)
-            if c + LOAD_AHEAD < CHUNKS:
-                sort_x(c + LOAD_AHEAD)
+            for i in range(TOKEN_TILES):
+                multiply(c, pieces, 0, n_banks, range(2 * i, 2 * i + 2))
+                if c + TURN_AHEAD < CHUNKS:
+                    turn_x(c + TURN_AHEAD, i)
+                if i == 0 and c + LOAD_AHEAD < CHUNKS:
+                    sort_x(c + LOAD_AHEAD)
             if c + TURN_AHEAD < CHUNKS:
-                turn_and_quantise_x(c + TURN_AHEAD)
+                quantise_x(c + TURN_AHEAD)
 
         early_mean = {}
         for i in range(TOKEN_TILES):

from contextlib import ExitStack

import concourse.mybir as mybir
from concourse.masks import make_identity

F32 = mybir.dt.float32
BF16 = mybir.dt.bfloat16
I32 = mybir.dt.int32
U32 = mybir.dt.uint32
U8 = mybir.dt.uint8
FP8X4 = mybir.dt.float8_e4m3fn_x4
ALU = mybir.AluOpType
ACT = mybir.ActivationFunctionType

P = 128
PACK = 4
K_PASS = P * PACK
TOKENS = 256
K = 16384
N = 1024
EPS = 1e-6

TOKEN_TILES = TOKENS // P
BANK = 512
N_BANKS = N // BANK
PASSES = K // K_PASS
CHUNK = 4
CHUNKS = PASSES // CHUNK
UNITS = TOKEN_TILES * CHUNK
SPLIT = 5
LOAD_AHEAD = 3
TURN_AHEAD = 2
QUADRANTS = 4
PLANE_ROWS = 4

HEADS = 8
PAIRS = 64
M = HEADS * PAIRS
M_BANK = BANK // 2
GRID = 8
FRAMES_PER_TILE = P // (GRID * GRID)
FRAME_PAIRS = 22
ROW_PAIRS = 43

FLOPS = 2 * TOKENS * K * N


def tile_causalwanselfattention_pa_k_kernel(
    tc, x, W_words, W_scales, b, g, freqs_cos, freqs_sin, out
):
    nc = tc.nc
    x_by_tile = x[0].rearrange("(i p) k -> p i k", p=P)
    out_rows = out[0].rearrange("l h d -> l (h d)")

    with ExitStack() as ctx:
        consts = ctx.enter_context(tc.tile_pool(name="consts", bufs=1))
        raw_pool = ctx.enter_context(tc.tile_pool(name="raw", bufs=3))
        stage_pool = ctx.enter_context(tc.tile_pool(name="stage", bufs=2))
        code_pool = ctx.enter_context(tc.tile_pool(name="codes", bufs=TURN_AHEAD + 2))
        w_pool = ctx.enter_context(tc.tile_pool(name="w", bufs=3 * CHUNK))
        tail_pool = ctx.enter_context(tc.tile_pool(name="tail", bufs=1))
        acc_pool = ctx.enter_context(tc.psum_pool(name="acc", bufs=1))
        bank_pool = ctx.enter_context(tc.psum_pool(name="bank", bufs=4))
        ctx.enter_context(tc.manual_schedule())

        w_scales = consts.tile([P, CHUNKS, N], U8, align_bytes=64)
        nc.vector.memset(w_scales[:].rearrange("p c n -> p (c n)").bitcast(I32), 0)
        bias_gain_row = consts.tile([P, 2 * N], BF16)
        nc.vector.memset(bias_gain_row[:], 0.0)
        freqs = consts.tile([P, 2 * PAIRS], BF16)
        nc.vector.memset(freqs[:], 0.0)
        nc.scalar.dma_start(out=bias_gain_row[0:1, 0:N], in_=b.unsqueeze(0))
        nc.scalar.dma_start(out=bias_gain_row[0:1, N : 2 * N], in_=g.unsqueeze(0))
        nc.scalar.dma_start(out=freqs[0:GRID, 0:PAIRS], in_=freqs_cos)
        nc.scalar.dma_start(out=freqs[0:GRID, PAIRS : 2 * PAIRS], in_=freqs_sin)
        ones = consts.tile([P, P], BF16)
        nc.vector.memset(ones[:], 1.0)
        one_column = consts.tile([P, 1], F32)
        nc.vector.memset(one_column[:], 1.0)
        sqrt_of_one = consts.tile([P, 1], F32)
        nc.scalar.activation(out=sqrt_of_one[:], in_=one_column[:], func=ACT.Sqrt)

        ident = consts.tile([P, P], F32)
        make_identity(nc, ident[:])

        for c in range(CHUNKS):
            for quadrant in range(QUADRANTS):
                first = 32 * quadrant
                rows = slice(PLANE_ROWS * quadrant, PLANE_ROWS * (quadrant + 1))
                nc.gpsimd.dma_start(
                    out=w_scales[first : first + CHUNK * PLANE_ROWS, c, :].bitcast(F32),
                    in_=W_scales[c * CHUNK : (c + 1) * CHUNK, rows, :].bitcast(F32),
                )

        select = consts.tile([P, 4, P], BF16)
        for i in range(TOKEN_TILES):
            nc.vector.tensor_copy(
                out=select[:, i, :].rearrange("p (f s) -> p f s", f=FRAMES_PER_TILE),
                in_=ident[:, FRAMES_PER_TILE * i : FRAMES_PER_TILE * (i + 1)]
                .unsqueeze(2)
                .to_broadcast([P, FRAMES_PER_TILE, GRID * GRID]),
            )
        nc.vector.tensor_copy(
            out=select[:, 2, :].rearrange("p (f r c) -> p f r c", f=FRAMES_PER_TILE, r=GRID),
            in_=ident[:, 0:GRID]
            .unsqueeze(1)
            .unsqueeze(3)
            .to_broadcast([P, FRAMES_PER_TILE, GRID, GRID]),
        )
        nc.vector.tensor_copy(
            out=select[:, 3, :].rearrange("p (s c) -> p s c", c=GRID),
            in_=ident[:, 0:GRID].unsqueeze(1).to_broadcast([P, P // GRID, GRID]),
        )

        acc = [
            [
                acc_pool.tile([P, BANK], F32, name="acc_%d_%d" % (i, h))
                for h in range(N_BANKS)
            ]
            for i in range(TOKEN_TILES)
        ]
        x_raw = {}
        x_sorted = {}
        grouped = {}
        x_codes = {}
        x_scales = {}

        def load_x(c):
            x_raw[c] = raw_pool.tile([P, TOKEN_TILES, CHUNK * K_PASS], BF16, name="x_raw")
            k_cols = slice(c * CHUNK * K_PASS, (c + 1) * CHUNK * K_PASS)
            nc.sync.dma_start(out=x_raw[c][:], in_=x_by_tile[:, :, k_cols])

        def sort_x(c):
            x_sorted[c] = stage_pool.tile([P, UNITS, 2, P], F32, name="x_sorted")
            nc.vector.tensor_copy(
                out=x_sorted[c][:],
                in_=x_raw[c][:]
                .rearrange("p i k -> p (i k)")
                .bitcast(F32)
                .rearrange("p (a w u) -> p a u w", a=UNITS, u=2),
            )

        def turn_x(c, i):
            if i == 0:
                grouped[c] = stage_pool.tile([P, UNITS, P, PACK], BF16, name="grouped", align_bytes=64)
            for half in range(2):
                first_unit = i * CHUNK + 2 * half
                turned = bank_pool.tile([P, 4, P], F32, tag="bank")
                for slot in range(4):
                    nc.tensor.transpose(
                        out=turned[:, slot, :],
                        in_=x_sorted[c][:, first_unit + slot // 2, slot % 2, :],
                        identity=ident[:],
                    )
                copy_out = nc.scalar.copy if half == 0 else nc.vector.tensor_copy
                copy_out(
                    out=grouped[c][:, first_unit : first_unit + 2, :, :].bitcast(F32),
                    in_=turned[:].rearrange("p (a u) r -> p a r u", u=2),
                )

        def quantise_x(c):
            x_codes[c] = code_pool.tile([P, UNITS, P], U32, name="x_codes", align_bytes=64)
            x_scales[c] = code_pool.tile([P, UNITS, P], U8, name="x_scales", align_bytes=64)
            nc.vector.quantize_mx(
                out=x_codes[c][:].rearrange("p a r -> p (a r)").bitcast(FP8X4),
                scales=x_scales[c][:].rearrange("p a r -> p (a r)"),
                in_=grouped[c][:].rearrange("p a r t -> p (a r t)"),
            )

        def load_w(c, first_bank, n_banks):
            byte_cols = slice(first_bank * PACK * BANK, (first_bank + n_banks) * PACK * BANK)
            pieces = []
            for k_pass in range(c * CHUNK, (c + 1) * CHUNK):
                piece = w_pool.tile([P, n_banks * PACK * BANK], U8, name="w_codes", align_bytes=64)
                nc.sync.dma_start(
                    out=piece[:].bitcast(I32),
                    in_=W_words[k_pass].rearrange("p n t -> p (n t)")[:, byte_cols].bitcast(I32),
                )
                pieces.append(piece)
            return pieces

        def multiply(c, pieces, first_bank, n_banks, passes=range(CHUNK)):
            for o in passes:
                k_pass = c * CHUNK + o
                for i in range(TOKEN_TILES):
                    unit = i * CHUNK + o
                    for local_bank in range(n_banks):
                        h = first_bank + local_bank
                        byte_cols = slice(local_bank * PACK * BANK, (local_bank + 1) * PACK * BANK)
                        nc.tensor.matmul_mx(
                            out=acc[i][h][:],
                            lhsT=x_codes[c][:, unit, :].bitcast(FP8X4),
                            lhsT_scale=x_scales[c][:, unit, :],
                            rhs=pieces[o][:, byte_cols].bitcast(FP8X4),
                            rhs_scale=w_scales[PLANE_ROWS * o : P, c, BANK * h : BANK * (h + 1)],
                            start=(k_pass == 0),
                            stop=(k_pass == PASSES - 1),
                        )

        bias_gain = consts.tile([P, 2, 2, M], F32)
        cos_sin = consts.tile([P, TOKEN_TILES, 3, PAIRS], F32)
        own_factor = consts.tile([P, TOKEN_TILES, 2, M], F32)
        partner_factor = consts.tile([P, TOKEN_TILES, 2, M], F32)

        def build_tables():
            for q in range(2 * N_BANKS):
                spread = bank_pool.tile([P, BANK], F32, tag="bank")
                nc.tensor.matmul(
                    out=spread[:],
                    lhsT=ones[:],
                    rhs=bias_gain_row[:, BANK * q : BANK * (q + 1)],
                    start=True,
                    stop=True,
                )
                half = q % N_BANKS
                nc.scalar.copy(
                    out=bias_gain[:, q // N_BANKS, :, M_BANK * half : M_BANK * (half + 1)],
                    in_=spread[:].rearrange("p (m e) -> p e m", e=2),
                )
            picked = bank_pool.tile([P, 4, 2, PAIRS], F32, tag="bank")
            for s in range(4):
                nc.tensor.matmul(
                    out=picked[:, s, :, :].rearrange("p s j -> p (s j)"),
                    lhsT=select[:, s, :],
                    rhs=freqs[:],
                    start=True,
                    stop=True,
                )
            gain = bias_gain[:, 1, :, :]
            for i in range(TOKEN_TILES):
                for s, first, last in (
                    (i, 0, FRAME_PAIRS),
                    (2, FRAME_PAIRS, ROW_PAIRS),
                    (3, ROW_PAIRS, PAIRS),
                ):
                    nc.vector.tensor_copy(
                        out=cos_sin[:, i, 0:2, first:last], in_=picked[:, s, :, first:last]
                    )
                nc.vector.tensor_scalar_mul(
                    out=cos_sin[:, i, 2, :], in0=cos_sin[:, i, 1, :], scalar1=-1.0
                )
                nc.vector.tensor_tensor(
                    out=own_factor[:, i, :, :].rearrange("p e (h j) -> p (e h) j", j=PAIRS),
                    in0=gain.rearrange("p e (h j) -> p (e h) j", j=PAIRS),
                    in1=cos_sin[:, i, 0:1, :].to_broadcast([P, 2 * HEADS, PAIRS]),
                    op=ALU.mult,
                )
                for e in range(2):
                    nc.vector.tensor_tensor(
                        out=partner_factor[:, i, e, :].rearrange("p (h j) -> p h j", j=PAIRS),
                        in0=gain[:, 1 - e, :].rearrange("p (h j) -> p h j", j=PAIRS),
                        in1=cos_sin[:, i, 2 - e : 3 - e, :].to_broadcast([P, HEADS, PAIRS]),
                        op=ALU.mult,
                    )

        y = {}
        sum_squares = {}
        own = {}
        rotated = {}
        inv_rms = {}

        def add_bias_and_square(i, h):
            pairs = slice(M_BANK * h, M_BANK * (h + 1))
            y[i, h] = tail_pool.tile([P, 2, M_BANK], F32, name="y_%d_%d" % (i, h))
            nc.vector.tensor_tensor(
                out=y[i, h][:],
                in0=acc[i][h][:].rearrange("p (m e) -> p e m", e=2),
                in1=bias_gain[:, 0, :, pairs],
                op=ALU.add,
            )
            squares = tail_pool.tile([P, BANK], F32, name="squares_%d_%d" % (i, h))
            sum_squares[i, h] = tail_pool.tile([P, 1], F32, name="sum_squares_%d_%d" % (i, h))
            nc.scalar.activation(
                out=squares[:],
                in_=y[i, h][:].rearrange("p e m -> p (e m)"),
                func=ACT.Square,
                accum_out=sum_squares[i, h][:],
            )

        def multiply_own(i, h):
            pairs = slice(M_BANK * h, M_BANK * (h + 1))
            own[i, h] = tail_pool.tile([P, 2, M_BANK], F32, name="own_%d_%d" % (i, h))
            nc.vector.tensor_tensor(
                out=own[i, h][:], in0=y[i, h][:], in1=own_factor[:, i, :, pairs], op=ALU.mult
            )

        def rotate(i, h, factor):
            pairs = slice(M_BANK * h, M_BANK * (h + 1))
            partner = tail_pool.tile([P, 2, M_BANK], F32, name="partner_%d_%d" % (i, h))
            for e in range(2):
                nc.vector.scalar_tensor_tensor(
                    out=partner[:, e, :],
                    in0=y[i, h][:, 1 - e, :],
                    scalar=factor,
                    in1=partner_factor[:, i, e, pairs],
                    op0=ALU.mult,
                    op1=ALU.mult,
                )
            rotated[i, h] = tail_pool.tile([P, BANK], F32, name="rotated_%d_%d" % (i, h))
            nc.vector.scalar_tensor_tensor(
                out=rotated[i, h][:].rearrange("p (m e) -> p m e", e=2),
                in0=own[i, h][:].rearrange("p e m -> p m e"),
                scalar=factor,
                in1=partner[:].rearrange("p e m -> p m e"),
                op0=ALU.mult,
                op1=ALU.add,
            )

        def store(i, h, result):
            nc.sync.dma_start(
                out=out_rows[P * i : P * (i + 1), BANK * h : BANK * (h + 1)], in_=result[:]
            )

        for c in range(LOAD_AHEAD):
            load_x(c)
        sort_x(0)
        for c in range(TURN_AHEAD):
            sort_x(c + 1)
            for i in range(TOKEN_TILES):
                turn_x(c, i)
            quantise_x(c)
        build_tables()

        for c in range(CHUNKS):
            n_banks = N_BANKS if c < SPLIT else 1
            pieces = load_w(c, 0, n_banks)
            if c + LOAD_AHEAD < CHUNKS:
                load_x(c + LOAD_AHEAD)
            for i in range(TOKEN_TILES):
                multiply(c, pieces, 0, n_banks, range(2 * i, 2 * i + 2))
                if c + TURN_AHEAD < CHUNKS:
                    turn_x(c + TURN_AHEAD, i)
                if i == 0 and c + LOAD_AHEAD < CHUNKS:
                    sort_x(c + LOAD_AHEAD)
            if c + TURN_AHEAD < CHUNKS:
                quantise_x(c + TURN_AHEAD)

        early_mean = {}
        for i in range(TOKEN_TILES):
            add_bias_and_square(i, 0)
        for i in range(TOKEN_TILES):
            multiply_own(i, 0)
            rotate(i, 0, 1.0)
            early_mean[i] = tail_pool.tile([P, 1], F32, name="early_mean_%d" % i)
            nc.vector.tensor_scalar(
                out=early_mean[i][:],
                in0=sum_squares[i, 0][:],
                scalar1=1.0 / N,
                scalar2=EPS,
                op0=ALU.mult,
                op1=ALU.add,
            )

        for c in range(SPLIT, CHUNKS):
            pieces = load_w(c, 1, 1)
            multiply(c, pieces, 1, 1)

        for i in range(TOKEN_TILES):
            add_bias_and_square(i, 1)
        for i in range(TOKEN_TILES):
            multiply_own(i, 1)
        for i in range(TOKEN_TILES):
            rms = tail_pool.tile([P, 1], F32, name="rms_%d" % i)
            nc.scalar.activation(
                out=rms[:],
                in_=sum_squares[i, 1][:],
                func=ACT.Sqrt,
                scale=1.0 / N,
                bias=early_mean[i][:],
            )
            inv_rms[i] = tail_pool.tile([P, 1], F32, name="inv_rms_%d" % i)
            nc.vector.reciprocal(out=inv_rms[i][:], in_=rms[:])
        for i in range(TOKEN_TILES):
            scaled = tail_pool.tile([P, BANK], F32, name="scaled_%d" % i)
            nc.scalar.activation(
                out=scaled[:], in_=rotated[i, 0][:], func=ACT.Copy, scale=inv_rms[i][:]
            )
            store(i, 0, scaled)
        for i in range(TOKEN_TILES):
            rotate(i, 1, inv_rms[i][:])
            store(i, 1, rotated[i, 1])
